import numpy as np
import ml_dtypes

BF16 = ml_dtypes.bfloat16


def bf(x):
    return np.asarray(x, np.float32).astype(BF16)


def f32(x):
    return np.asarray(x, np.float32)


def f64(x):
    return np.asarray(x).astype(np.float64)


def striped(idx):
    return np.tile(idx.reshape(-1, 16).T, (8, 1))


R, T, C, NB, N, S = 4, 16, 256, 32, 512, 4096

H4 = np.array([[1, 1, 1, 1], [1, -1, 1, -1], [1, 1, -1, -1], [1, -1, -1, 1]], np.float64)


def setup_inputs():
    return {"trans": f32(2.0 * np.random.standard_normal((C, N))), "bias": f32(0.2 * np.random.standard_normal((C, 1))), "base": f32(np.random.standard_normal((C, S))), "offs": striped(np.random.permutation(S)[:N])}


def reference(trans, bias, base, offs):
    idx = offs[:16].T.reshape(-1)
    y = f64(trans).reshape(C, R, R, NB)
    z = np.einsum("pu,qv,cuvn->cpqn", H4, H4, y) / T
    out = f64(base).copy()
    out[:, idx] = z.reshape(C, N) + f64(bias)
    return out

@@ -1,0 +1,68 @@
+import concourse.mybir as mybir
+
+F32 = mybir.dt.float32
+U16 = mybir.dt.uint16
+ADD = mybir.AluOpType.add
+SUBTRACT = mybir.AluOpType.subtract
+COPY = mybir.ActivationFunctionType.Copy
+
+P = 128
+C = 256
+T = 16
+NB = 32
+N = T * NB
+S = 4096
+HALF = S // 2
+
+
+def butterfly(nc, dst, src, run):
+    pairs_in = src[:].rearrange("p (h two l) -> p h two l", two=2, l=run)
+    pairs_out = dst[:].rearrange("p (h two l) -> p h two l", two=2, l=run)
+    nc.vector.tensor_tensor(pairs_out[:, :, 0, :], pairs_in[:, :, 0, :], pairs_in[:, :, 1, :], ADD)
+    nc.vector.tensor_tensor(pairs_out[:, :, 1, :], pairs_in[:, :, 0, :], pairs_in[:, :, 1, :], SUBTRACT)
+
+
+def tile_iwht3layer_kernel(tc, trans, bias, base, offs, out):
+    nc = tc.nc
+    channel_blocks = range(C // P)
+    with tc.tile_pool(name="held", bufs=1) as held:
+        offsets = held.tile([P, N // 16], U16, name="offsets")
+        nc.sync.dma_start(offsets[:], offs)
+        coeffs = [held.tile([P, N], F32, name=f"coeffs{b}") for b in channel_blocks]
+        shifts = [held.tile([P, 1], F32, name=f"shift{b}") for b in channel_blocks]
+        windows = [held.tile([P, S], F32, name=f"window{b}") for b in channel_blocks]
+        nc.sync.dma_start(coeffs[0][:], trans[0:P, :])
+        nc.scalar.dma_start(coeffs[1][:], trans[P : 2 * P, :])
+        for b in channel_blocks:
+            nc.scalar.dma_start(shifts[b][:], bias[b * P : (b + 1) * P, :])
+        for b in channel_blocks:
+            rows = slice(b * P, (b + 1) * P)
+            nc.sync.dma_start(windows[b][:, :HALF], base[rows, :HALF])
+            nc.scalar.dma_start(windows[b][:, HALF:], base[rows, HALF:])
+
+        bias_planes = []
+        for b in channel_blocks:
+            plane = held.tile([P, N], F32, name=f"bias_plane{b}")
+            nc.scalar.activation(plane[:], shifts[b][:, 0:1].to_broadcast([P, N]), COPY)
+            bias_planes.append(plane)
+
+        pixels = []
+        for b in channel_blocks:
+            stage = held.tile([P, N], F32, name=f"scaled{b}")
+            nc.vector.tensor_scalar_mul(stage[:], coeffs[b][:], 1.0 / T)
+            for k in range(4):
+                after = held.tile([P, N], F32, name=f"layer{k}_{b}")
+                butterfly(nc, after, stage, NB << k)
+                stage = after
+            pixels.append(stage)
+
+        for b in channel_blocks:
+            rows = slice(b * P, (b + 1) * P)
+            nc.vector.tensor_tensor(
+                windows[b][:].indirect(offsets[:]),
+                pixels[b][:],
+                bias_planes[b][:],
+                ADD,
+            )
+            nc.sync.dma_start(out[rows, :HALF], windows[b][:, :HALF])
+            nc.scalar.dma_start(out[rows, HALF:], windows[b][:, HALF:])

@@ -4,7 +4,7 @@ F32 = mybir.dt.float32
 U16 = mybir.dt.uint16
 ADD = mybir.AluOpType.add
 SUBTRACT = mybir.AluOpType.subtract
-COPY = mybir.ActivationFunctionType.Copy
+IDENTITY = mybir.ActivationFunctionType.Identity
 
 P = 128
 C = 256
@@ -12,7 +12,8 @@ T = 16
 NB = 32
 N = T * NB
 S = 4096
-HALF = S // 2
+HALF_S = S // 2
+HALF_N = N // 2
 
 
 def butterfly(nc, dst, src, run):
@@ -37,32 +38,36 @@ def tile_iwht3layer_kernel(tc, trans, bias, base, offs, out):
             nc.scalar.dma_start(shifts[b][:], bias[b * P : (b + 1) * P, :])
         for b in channel_blocks:
             rows = slice(b * P, (b + 1) * P)
-            nc.sync.dma_start(windows[b][:, :HALF], base[rows, :HALF])
-            nc.scalar.dma_start(windows[b][:, HALF:], base[rows, HALF:])
+            nc.sync.dma_start(windows[b][:, :HALF_S], base[rows, :HALF_S])
+            nc.scalar.dma_start(windows[b][:, HALF_S:], base[rows, HALF_S:])
 
-        bias_planes = []
+        low_twice, high_signed = [], []
         for b in channel_blocks:
-            plane = held.tile([P, N], F32, name=f"bias_plane{b}")
-            nc.scalar.activation(plane[:], shifts[b][:, 0:1].to_broadcast([P, N]), COPY)
-            bias_planes.append(plane)
-
-        pixels = []
-        for b in channel_blocks:
-            stage = held.tile([P, N], F32, name=f"scaled{b}")
-            nc.vector.tensor_scalar_mul(stage[:], coeffs[b][:], 1.0 / T)
-            for k in range(4):
+            stage = coeffs[b]
+            for k in range(3):
                 after = held.tile([P, N], F32, name=f"layer{k}_{b}")
                 butterfly(nc, after, stage, NB << k)
                 stage = after
-            pixels.append(stage)
+            low, high = stage[:, :HALF_N], stage[:, HALF_N:]
+
+            first = held.tile([P, N], F32, name=f"low_twice{b}")
+            nc.scalar.activation(
+                first[:].rearrange("p (r j) -> p r j", r=2),
+                low.unsqueeze(1).to_broadcast([P, 2, HALF_N]),
+                IDENTITY,
+                bias=shifts[b][:, 0:1],
+                scale=1.0 / T,
+            )
+            second = held.tile([P, N], F32, name=f"high_signed{b}")
+            nc.scalar.mul(second[:, :HALF_N], high, 1.0 / T)
+            nc.scalar.mul(second[:, HALF_N:], high, -1.0 / T)
+            low_twice.append(first)
+            high_signed.append(second)
 
         for b in channel_blocks:
             rows = slice(b * P, (b + 1) * P)
             nc.vector.tensor_tensor(
-                windows[b][:].indirect(offsets[:]),
-                pixels[b][:],
-                bias_planes[b][:],
-                ADD,
+                windows[b][:].indirect(offsets[:]), low_twice[b][:], high_signed[b][:], ADD
             )
-            nc.sync.dma_start(out[rows, :HALF], windows[b][:, :HALF])
-            nc.scalar.dma_start(out[rows, HALF:], windows[b][:, HALF:])
+            nc.sync.dma_start(out[rows, :HALF_S], windows[b][:, :HALF_S])
+            nc.scalar.dma_start(out[rows, HALF_S:], windows[b][:, HALF_S:])

@@ -31,21 +31,22 @@ def tile_iwht3layer_kernel(tc, trans, bias, base, offs, out):
         nc.sync.dma_start(offsets[:], offs)
         coeffs = [held.tile([P, N], F32, name=f"coeffs{b}") for b in channel_blocks]
         shifts = [held.tile([P, 1], F32, name=f"shift{b}") for b in channel_blocks]
-        windows = [held.tile([P, S], F32, name=f"window{b}") for b in channel_blocks]
         nc.sync.dma_start(coeffs[0][:], trans[0:P, :])
         nc.scalar.dma_start(coeffs[1][:], trans[P : 2 * P, :])
         for b in channel_blocks:
             nc.scalar.dma_start(shifts[b][:], bias[b * P : (b + 1) * P, :])
+
+        windows, low_twice, high_signed = [], [], []
         for b in channel_blocks:
             rows = slice(b * P, (b + 1) * P)
-            nc.sync.dma_start(windows[b][:, :HALF_S], base[rows, :HALF_S])
-            nc.scalar.dma_start(windows[b][:, HALF_S:], base[rows, HALF_S:])
+            window = held.tile([P, S], F32, name=f"window{b}", tag="turn" if b == 1 else "window0")
+            nc.sync.dma_start(window[:, :HALF_S], base[rows, :HALF_S])
+            nc.scalar.dma_start(window[:, HALF_S:], base[rows, HALF_S:])
+            windows.append(window)
 
-        low_twice, high_signed = [], []
-        for b in channel_blocks:
             stage = coeffs[b]
             for k in range(3):
-                after = held.tile([P, N], F32, name=f"layer{k}_{b}")
+                after = held.tile([P, N], F32, name=f"layer{k}_{b}", tag="turn" if (b, k) == (0, 1) else f"layer{k}_{b}")
                 butterfly(nc, after, stage, NB << k)
                 stage = after
             low, high = stage[:, :HALF_N], stage[:, HALF_N:]

@@ -31,22 +31,19 @@ def tile_iwht3layer_kernel(tc, trans, bias, base, offs, out):
         nc.sync.dma_start(offsets[:], offs)
         coeffs = [held.tile([P, N], F32, name=f"coeffs{b}") for b in channel_blocks]
         shifts = [held.tile([P, 1], F32, name=f"shift{b}") for b in channel_blocks]
+        windows = [held.tile([P, S], F32, name=f"window{b}") for b in channel_blocks]
         nc.sync.dma_start(coeffs[0][:], trans[0:P, :])
-        nc.scalar.dma_start(coeffs[1][:], trans[P : 2 * P, :])
+        nc.sync.dma_start(coeffs[1][:], trans[P : 2 * P, :])
         for b in channel_blocks:
             nc.scalar.dma_start(shifts[b][:], bias[b * P : (b + 1) * P, :])
-
-        windows, low_twice, high_signed = [], [], []
         for b in channel_blocks:
-            rows = slice(b * P, (b + 1) * P)
-            window = held.tile([P, S], F32, name=f"window{b}", tag="turn" if b == 1 else "window0")
-            nc.sync.dma_start(window[:, :HALF_S], base[rows, :HALF_S])
-            nc.scalar.dma_start(window[:, HALF_S:], base[rows, HALF_S:])
-            windows.append(window)
+            nc.sync.dma_start(windows[b][:], base[b * P : (b + 1) * P, :])
 
+        low_twice, high_signed = [], []
+        for b in channel_blocks:
             stage = coeffs[b]
             for k in range(3):
-                after = held.tile([P, N], F32, name=f"layer{k}_{b}", tag="turn" if (b, k) == (0, 1) else f"layer{k}_{b}")
+                after = held.tile([P, N], F32, name=f"layer{k}_{b}")
                 butterfly(nc, after, stage, NB << k)
                 stage = after
             low, high = stage[:, :HALF_N], stage[:, HALF_N:]

@@ -29,15 +29,17 @@ def tile_iwht3layer_kernel(tc, trans, bias, base, offs, out):
     with tc.tile_pool(name="held", bufs=1) as held:
         offsets = held.tile([P, N // 16], U16, name="offsets")
         nc.sync.dma_start(offsets[:], offs)
+        shifts = held.tile([P, C // P], F32, name="shifts")
+        with nc.allow_non_contiguous_dma(reason="256 single floats, one or two to a partition"):
+            nc.scalar.dma_start(shifts[:], bias.rearrange("(b p) one -> p (b one)", p=P))
         coeffs = [held.tile([P, N], F32, name=f"coeffs{b}") for b in channel_blocks]
-        shifts = [held.tile([P, 1], F32, name=f"shift{b}") for b in channel_blocks]
         windows = [held.tile([P, S], F32, name=f"window{b}") for b in channel_blocks]
         nc.sync.dma_start(coeffs[0][:], trans[0:P, :])
-        nc.sync.dma_start(coeffs[1][:], trans[P : 2 * P, :])
+        nc.scalar.dma_start(coeffs[1][:], trans[P : 2 * P, :])
         for b in channel_blocks:
-            nc.scalar.dma_start(shifts[b][:], bias[b * P : (b + 1) * P, :])
-        for b in channel_blocks:
-            nc.sync.dma_start(windows[b][:], base[b * P : (b + 1) * P, :])
+            rows = slice(b * P, (b + 1) * P)
+            nc.sync.dma_start(windows[b][:, :HALF_S], base[rows, :HALF_S])
+            nc.scalar.dma_start(windows[b][:, HALF_S:], base[rows, HALF_S:])
 
         low_twice, high_signed = [], []
         for b in channel_blocks:
@@ -53,7 +55,7 @@ def tile_iwht3layer_kernel(tc, trans, bias, base, offs, out):
                 first[:].rearrange("p (r j) -> p r j", r=2),
                 low.unsqueeze(1).to_broadcast([P, 2, HALF_N]),
                 IDENTITY,
-                bias=shifts[b][:, 0:1],
+                bias=shifts[:, b : b + 1],
                 scale=1.0 / T,
             )
             second = held.tile([P, N], F32, name=f"high_signed{b}")

@@ -12,7 +12,6 @@ T = 16
 NB = 32
 N = T * NB
 S = 4096
-HALF_S = S // 2
 HALF_N = N // 2
 
 
@@ -28,18 +27,17 @@ def tile_iwht3layer_kernel(tc, trans, bias, base, offs, out):
     channel_blocks = range(C // P)
     with tc.tile_pool(name="held", bufs=1) as held:
         offsets = held.tile([P, N // 16], U16, name="offsets")
-        nc.sync.dma_start(offsets[:], offs)
-        shifts = held.tile([P, C // P], F32, name="shifts")
-        with nc.allow_non_contiguous_dma(reason="256 single floats, one or two to a partition"):
-            nc.scalar.dma_start(shifts[:], bias.rearrange("(b p) one -> p (b one)", p=P))
         coeffs = [held.tile([P, N], F32, name=f"coeffs{b}") for b in channel_blocks]
+        shifts = [held.tile([P, 1], F32, name=f"shift{b}") for b in channel_blocks]
         windows = [held.tile([P, S], F32, name=f"window{b}") for b in channel_blocks]
-        nc.sync.dma_start(coeffs[0][:], trans[0:P, :])
-        nc.scalar.dma_start(coeffs[1][:], trans[P : 2 * P, :])
+
+        nc.sync.dma_start(offsets[:], offs)
         for b in channel_blocks:
-            rows = slice(b * P, (b + 1) * P)
-            nc.sync.dma_start(windows[b][:, :HALF_S], base[rows, :HALF_S])
-            nc.scalar.dma_start(windows[b][:, HALF_S:], base[rows, HALF_S:])
+            nc.sync.dma_start(coeffs[b][:], trans[b * P : (b + 1) * P, :])
+        for b in channel_blocks:
+            nc.sync.dma_start(windows[b][:], base[b * P : (b + 1) * P, :])
+        for b in channel_blocks:
+            nc.scalar.dma_start(shifts[b][:], bias[b * P : (b + 1) * P, :])
 
         low_twice, high_signed = [], []
         for b in channel_blocks:
@@ -55,7 +53,7 @@ def tile_iwht3layer_kernel(tc, trans, bias, base, offs, out):
                 first[:].rearrange("p (r j) -> p r j", r=2),
                 low.unsqueeze(1).to_broadcast([P, 2, HALF_N]),
                 IDENTITY,
-                bias=shifts[:, b : b + 1],
+                bias=shifts[b][:, 0:1],
                 scale=1.0 / T,
             )
             second = held.tile([P, N], F32, name=f"high_signed{b}")
@@ -65,9 +63,7 @@ def tile_iwht3layer_kernel(tc, trans, bias, base, offs, out):
             high_signed.append(second)
 
         for b in channel_blocks:
-            rows = slice(b * P, (b + 1) * P)
             nc.vector.tensor_tensor(
                 windows[b][:].indirect(offsets[:]), low_twice[b][:], high_signed[b][:], ADD
             )
-            nc.sync.dma_start(out[rows, :HALF_S], windows[b][:, :HALF_S])
-            nc.scalar.dma_start(out[rows, HALF_S:], windows[b][:, HALF_S:])
+            nc.sync.dma_start(out[b * P : (b + 1) * P, :], windows[b][:])

@@ -25,7 +25,7 @@ def butterfly(nc, dst, src, run):
 def tile_iwht3layer_kernel(tc, trans, bias, base, offs, out):
     nc = tc.nc
     channel_blocks = range(C // P)
-    with tc.tile_pool(name="held", bufs=1) as held:
+    with tc.tile_pool(name="held", bufs=1) as held, tc.psum_pool(name="psum", bufs=1) as psum:
         offsets = held.tile([P, N // 16], U16, name="offsets")
         coeffs = [held.tile([P, N], F32, name=f"coeffs{b}") for b in channel_blocks]
         shifts = [held.tile([P, 1], F32, name=f"shift{b}") for b in channel_blocks]
@@ -36,8 +36,14 @@ def tile_iwht3layer_kernel(tc, trans, bias, base, offs, out):
             nc.sync.dma_start(coeffs[b][:], trans[b * P : (b + 1) * P, :])
         for b in channel_blocks:
             nc.sync.dma_start(windows[b][:], base[b * P : (b + 1) * P, :])
+        bias_row = held.tile([1, C], F32, name="bias_row")
+        nc.scalar.dma_start(bias_row[:], bias.rearrange("c one -> one c"))
+        unit = held.tile([1, 1], F32, name="unit")
+        nc.vector.memset(unit[:], 1.0)
         for b in channel_blocks:
-            nc.scalar.dma_start(shifts[b][:], bias[b * P : (b + 1) * P, :])
+            column = psum.tile([P, 1], F32, name=f"column{b}")
+            nc.tensor.matmul(column[:], bias_row[:, b * P : (b + 1) * P], unit[:], start=True, stop=True)
+            nc.vector.tensor_copy(shifts[b][:], column[:])
 
         low_twice, high_signed = [], []
         for b in channel_blocks:

@@ -16,8 +16,8 @@ HALF_N = N // 2
 
 
 def butterfly(nc, dst, src, run):
-    pairs_in = src[:].rearrange("p (h two l) -> p h two l", two=2, l=run)
-    pairs_out = dst[:].rearrange("p (h two l) -> p h two l", two=2, l=run)
+    pairs_in = src.rearrange("p (h two l) -> p h two l", two=2, l=run)
+    pairs_out = dst.rearrange("p (h two l) -> p h two l", two=2, l=run)
     nc.vector.tensor_tensor(pairs_out[:, :, 0, :], pairs_in[:, :, 0, :], pairs_in[:, :, 1, :], ADD)
     nc.vector.tensor_tensor(pairs_out[:, :, 1, :], pairs_in[:, :, 0, :], pairs_in[:, :, 1, :], SUBTRACT)
 
@@ -27,31 +27,32 @@ def tile_iwht3layer_kernel(tc, trans, bias, base, offs, out):
     channel_blocks = range(C // P)
     with tc.tile_pool(name="held", bufs=1) as held, tc.psum_pool(name="psum", bufs=1) as psum:
         offsets = held.tile([P, N // 16], U16, name="offsets")
-        coeffs = [held.tile([P, N], F32, name=f"coeffs{b}") for b in channel_blocks]
+        coeffs = held.tile([P, C // P, N], F32, name="coeffs")
         shifts = [held.tile([P, 1], F32, name=f"shift{b}") for b in channel_blocks]
         windows = [held.tile([P, S], F32, name=f"window{b}") for b in channel_blocks]
 
+        base_blocks = base.rearrange("(p b) s -> b p s", p=P)
+        out_blocks = out.rearrange("(p b) s -> b p s", p=P)
         nc.sync.dma_start(offsets[:], offs)
+        nc.sync.dma_start(coeffs[:], trans.rearrange("(p b) n -> p b n", p=P))
         for b in channel_blocks:
-            nc.sync.dma_start(coeffs[b][:], trans[b * P : (b + 1) * P, :])
-        for b in channel_blocks:
-            nc.sync.dma_start(windows[b][:], base[b * P : (b + 1) * P, :])
+            nc.sync.dma_start(windows[b][:], base_blocks[b])
         bias_row = held.tile([1, C], F32, name="bias_row")
         nc.scalar.dma_start(bias_row[:], bias.rearrange("c one -> one c"))
         unit = held.tile([1, 1], F32, name="unit")
         nc.vector.memset(unit[:], 1.0)
         for b in channel_blocks:
             column = psum.tile([P, 1], F32, name=f"column{b}")
-            nc.tensor.matmul(column[:], bias_row[:, b * P : (b + 1) * P], unit[:], start=True, stop=True)
+            nc.tensor.matmul(column[:], bias_row[:, b : C : C // P], unit[:], start=True, stop=True)
             nc.vector.tensor_copy(shifts[b][:], column[:])
 
         low_twice, high_signed = [], []
         for b in channel_blocks:
-            stage = coeffs[b]
+            stage = coeffs[:, b, :]
             for k in range(3):
                 after = held.tile([P, N], F32, name=f"layer{k}_{b}")
-                butterfly(nc, after, stage, NB << k)
-                stage = after
+                butterfly(nc, after[:], stage, NB << k)
+                stage = after[:]
             low, high = stage[:, :HALF_N], stage[:, HALF_N:]
 
             first = held.tile([P, N], F32, name=f"low_twice{b}")
@@ -72,4 +73,4 @@ def tile_iwht3layer_kernel(tc, trans, bias, base, offs, out):
             nc.vector.tensor_tensor(
                 windows[b][:].indirect(offsets[:]), low_twice[b][:], high_signed[b][:], ADD
             )
-            nc.sync.dma_start(out[b * P : (b + 1) * P, :], windows[b][:])
+            nc.sync.dma_start(out_blocks[b], windows[b][:])

@@ -13,6 +13,7 @@ NB = 32
 N = T * NB
 S = 4096
 HALF_N = N // 2
+BURST = 256
 
 
 def butterfly(nc, dst, src, run):
@@ -29,7 +30,7 @@ def tile_iwht3layer_kernel(tc, trans, bias, base, offs, out):
         offsets = held.tile([P, N // 16], U16, name="offsets")
         coeffs = held.tile([P, C // P, N], F32, name="coeffs")
         shifts = [held.tile([P, 1], F32, name=f"shift{b}") for b in channel_blocks]
-        windows = [held.tile([P, S], F32, name=f"window{b}") for b in channel_blocks]
+        windows = [held.tile([P, S], F32, name=f"window{b}", align_bytes=BURST) for b in channel_blocks]
 
         base_blocks = base.rearrange("(p b) s -> b p s", p=P)
         out_blocks = out.rearrange("(p b) s -> b p s", p=P)

import concourse.mybir as mybir

F32 = mybir.dt.float32
U16 = mybir.dt.uint16
ADD = mybir.AluOpType.add
SUBTRACT = mybir.AluOpType.subtract
IDENTITY = mybir.ActivationFunctionType.Identity

P = 128
C = 256
T = 16
NB = 32
N = T * NB
S = 4096
HALF_N = N // 2
BURST = 256


def butterfly(nc, dst, src, run):
    pairs_in = src.rearrange("p (h two l) -> p h two l", two=2, l=run)
    pairs_out = dst.rearrange("p (h two l) -> p h two l", two=2, l=run)
    nc.vector.tensor_tensor(pairs_out[:, :, 0, :], pairs_in[:, :, 0, :], pairs_in[:, :, 1, :], ADD)
    nc.vector.tensor_tensor(pairs_out[:, :, 1, :], pairs_in[:, :, 0, :], pairs_in[:, :, 1, :], SUBTRACT)


def tile_iwht3layer_kernel(tc, trans, bias, base, offs, out):
    nc = tc.nc
    channel_blocks = range(C // P)
    with tc.tile_pool(name="held", bufs=1) as held, tc.psum_pool(name="psum", bufs=1) as psum:
        offsets = held.tile([P, N // 16], U16, name="offsets")
        coeffs = held.tile([P, C // P, N], F32, name="coeffs")
        shifts = [held.tile([P, 1], F32, name=f"shift{b}") for b in channel_blocks]
        windows = [held.tile([P, S], F32, name=f"window{b}", align_bytes=BURST) for b in channel_blocks]

        base_blocks = base.rearrange("(p b) s -> b p s", p=P)
        out_blocks = out.rearrange("(p b) s -> b p s", p=P)
        nc.sync.dma_start(offsets[:], offs)
        nc.sync.dma_start(coeffs[:], trans.rearrange("(p b) n -> p b n", p=P))
        for b in channel_blocks:
            nc.sync.dma_start(windows[b][:], base_blocks[b])
        bias_row = held.tile([1, C], F32, name="bias_row")
        nc.scalar.dma_start(bias_row[:], bias.rearrange("c one -> one c"))
        unit = held.tile([1, 1], F32, name="unit")
        nc.vector.memset(unit[:], 1.0)
        for b in channel_blocks:
            column = psum.tile([P, 1], F32, name=f"column{b}")
            nc.tensor.matmul(column[:], bias_row[:, b : C : C // P], unit[:], start=True, stop=True)
            nc.vector.tensor_copy(shifts[b][:], column[:])

        low_twice, high_signed = [], []
        for b in channel_blocks:
            stage = coeffs[:, b, :]
            for k in range(3):
                after = held.tile([P, N], F32, name=f"layer{k}_{b}")
                butterfly(nc, after[:], stage, NB << k)
                stage = after[:]
            low, high = stage[:, :HALF_N], stage[:, HALF_N:]

            first = held.tile([P, N], F32, name=f"low_twice{b}")
            nc.scalar.activation(
                first[:].rearrange("p (r j) -> p r j", r=2),
                low.unsqueeze(1).to_broadcast([P, 2, HALF_N]),
                IDENTITY,
                bias=shifts[b][:, 0:1],
                scale=1.0 / T,
            )
            second = held.tile([P, N], F32, name=f"high_signed{b}")
            nc.scalar.mul(second[:, :HALF_N], high, 1.0 / T)
            nc.scalar.mul(second[:, HALF_N:], high, -1.0 / T)
            low_twice.append(first)
            high_signed.append(second)

        for b in channel_blocks:
            nc.vector.tensor_tensor(
                windows[b][:].indirect(offsets[:]), low_twice[b][:], high_signed[b][:], ADD
            )
            nc.sync.dma_start(out_blocks[b], windows[b][:])
